import numpy as np
import ml_dtypes


def mxq(x, axis, fmt="e4m3"):
    dtype, down = {"e4m3": (ml_dtypes.float8_e4m3fn, 7), "e5m2": (ml_dtypes.float8_e5m2, 14)}[fmt]
    v = np.moveaxis(np.asarray(x, np.float32).astype(ml_dtypes.bfloat16).astype(np.float64), axis, -1)
    blocks = v.reshape(v.shape[:-1] + (-1, 32))
    amax = np.abs(blocks).max(-1, keepdims=True)
    byte = np.maximum(np.where(amax > 0, np.frexp(amax)[1] - 1 + 127, 0) - down, 1)
    scale = np.exp2(byte - 127.0)
    codes = (blocks / scale).astype(np.float32).astype(dtype).astype(np.float64)
    return np.moveaxis((codes * scale).reshape(v.shape), -1, axis)


WIDE = False


def mx_kscale(k):
    if not WIDE:
        return np.ones(k)
    levels = np.array([10, -10, 5, -5, 0])
    if k % 512:
        return np.exp2(np.random.permutation(np.resize(levels, k // 32))).repeat(32)
    a = np.empty((k // 512, 16))
    for p in range(k // 512):
        a[p, :8] = np.random.permutation(np.resize(levels, 8))
        for g in range(8):
            far = levels[np.abs(levels - a[p, g]) >= 10]
            a[p, g + 8] = far[np.random.randint(len(far))]
    return np.exp2(a.ravel()).repeat(32)


BF16 = ml_dtypes.bfloat16


def bf(x):
    return np.asarray(x, np.float32).astype(BF16)


def f64(x):
    return np.asarray(x).astype(np.float64)


B, N0, N1, N2, N3, T, K = 256, 512, 1024, 1024, 512, 8, 512
R = min(K, N0, N1)
R2 = min(R, T)
GS = 0.25


def setup_inputs():
    s, t = mx_kscale(R), mx_kscale(R)
    return {"S": bf(np.random.standard_normal((R, R, R2)) * s[:, None, None] * t[None, :, None]),
            "U0": bf(np.random.standard_normal((N1, R)) / np.sqrt(R) / s[None, :]),
            "U1": bf(np.random.standard_normal((N0, R)) * GS / np.sqrt(R) / t[None, :])}


def reference(S, U0, U1):
    w1 = mxq(f64(S).reshape(R, R * R2).T, 1, "e4m3") @ mxq(f64(U0).T, 0, "e4m3")
    w2 = mxq(w1.reshape(R, R2 * N1).T, 1, "e4m3") @ mxq(f64(U1).T, 0, "e4m3")
    return w2.reshape(R2, N1, N0)

@@ -1,0 +1,196 @@
+from contextlib import ExitStack
+
+import concourse.masks as masks
+import concourse.mybir as mybir
+
+F32 = mybir.dt.float32
+BF16 = mybir.dt.bfloat16
+U32 = mybir.dt.uint32
+U8 = mybir.dt.uint8
+FP8X4 = mybir.dt.float8_e4m3fn_x4
+
+BANK_DT = F32
+
+P = 128
+N_R = 8
+N_A = 8
+N_UNITS = 16
+FLOPS = 2 * 512 * 4096 * 1024 + 2 * 512 * 8192 * 512
+
+S_CHUNK_M = (32, 32, 32, 16, 16)
+
+
+def tile_mtl_net_tf_pa_kernel(tc, S, U0, U1, out):
+    nc = tc.nc
+    with ExitStack() as ctx:
+        keep = ctx.enter_context(tc.tile_pool(name="keep", bufs=1))
+        wpool = ctx.enter_context(tc.tile_pool(name="wpool", bufs=3))
+        opool = ctx.enter_context(tc.tile_pool(name="opool", bufs=4))
+        ps1 = ctx.enter_context(tc.psum_pool(name="ps1", bufs=4))
+        ps2 = ctx.enter_context(tc.psum_pool(name="ps2", bufs=4))
+
+        def copy_on(engine, dst, src):
+            if engine == "v":
+                nc.vector.tensor_copy(out=dst, in_=src)
+            else:
+                nc.scalar.copy(out=dst, in_=src)
+
+        u0_view = U0.rearrange("(m a) q -> m a q", a=N_A)
+        u0_raw = []
+        for h in range(2):
+            t_raw = keep.tile([P, 4, 512], BF16, name="u0_raw%d" % h)
+            nc.sync.dma_start(out=t_raw[:], in_=u0_view[:, 4 * h : 4 * h + 4, :])
+            u0_raw.append(t_raw)
+        s_view = S.rearrange("(k j) p r -> k j (p r)", j=4)
+        s_raw = []
+        u1_raw = keep.tile([P, 4, 512], BF16, name="u1_raw")
+        m0 = 0
+        for k, mc in enumerate(S_CHUNK_M):
+            t_raw = keep.tile([P, 4, 32 * mc], BF16, name="s_raw%d" % k)
+            nc.sync.dma_start(out=t_raw[:], in_=s_view[:, :, 32 * m0 : 32 * (m0 + mc)])
+            s_raw.append(t_raw)
+            m0 += mc
+        nc.sync.dma_start(out=u1_raw[:], in_=U1.rearrange("(b m) k -> m b k", b=4))
+
+        ident = keep.tile([P, P], F32, name="ident")
+        masks.make_identity(nc, ident[:])
+        warm_in = keep.tile([P, 8], F32, name="warm_in")
+        warm_out = keep.tile([P, 8], F32, name="warm_out")
+        nc.vector.memset(warm_in[:], 0.0)
+        nc.scalar.copy(out=warm_out[:], in_=warm_in[:])
+
+        def prepare_factor(raw, label):
+            words = raw[:].bitcast(F32)
+            grouped = keep.tile([P, 4, P, 4], BF16, name="grp_" + label, align_bytes=64)
+            grouped_words = grouped[:].bitcast(F32)
+            for pair in range(2):
+                xt = ps2.tile([P, 2, 2, P], F32, name="xt", tag="acc2")
+                for s in range(2):
+                    for u in range(2):
+                        nc.tensor.transpose(xt[:, s, u, :], words[:, 2 * pair + s, u:256:2], ident[:])
+                nc.scalar.copy(
+                    out=grouped_words[:, 2 * pair : 2 * pair + 2, :, :],
+                    in_=xt[:].rearrange("p s u m -> p s m u"),
+                )
+            codes = keep.tile([P, 512], U32, name="codes_" + label, align_bytes=64)
+            scales = keep.tile([P, 512], U8, name="scales_" + label, align_bytes=64)
+            nc.vector.quantize_mx(
+                out=codes[:].bitcast(FP8X4),
+                scales=scales[:],
+                in_=grouped[:].rearrange("p s m t -> p (s m t)"),
+            )
+            return codes, scales
+
+        u0_q = [prepare_factor(u0_raw[0], "u0a"), prepare_factor(u0_raw[1], "u0b")]
+
+        s_grp = [keep.tile([P, 4, 4, P, 4], BF16, name="s_grp%d" % rh, align_bytes=64) for rh in range(2)]
+        m0 = 0
+        for k, mc in enumerate(S_CHUNK_M):
+            src5 = s_raw[k][:].rearrange("p j (m t r) -> p j m t r", t=4, r=N_R)
+            for rh in range(2):
+                for t in range(4):
+                    engine = "s" if (t == 3 or (t == 2 and rh == 1 and k % 2 == 0)) else "v"
+                    copy_on(
+                        engine,
+                        s_grp[rh][:, :, t, m0 : m0 + mc, :].rearrange("p r m j -> p m r j"),
+                        src5[:, :, :, t, 4 * rh : 4 * rh + 4].rearrange("p j m r -> p m r j"),
+                    )
+            m0 += mc
+
+        s_q = {}
+
+        def quantize_s(r):
+            codes = keep.tile([P, 512], U32, name="s_codes%d" % r, align_bytes=64)
+            scales = keep.tile([P, 512], U8, name="s_scales%d" % r, align_bytes=64)
+            nc.vector.quantize_mx(
+                out=codes[:].bitcast(FP8X4),
+                scales=scales[:],
+                in_=s_grp[r // 4][:, r % 4, :, :, :].rearrange("p t m j -> p (t m j)"),
+            )
+            s_q[r] = (codes, scales)
+
+        w_bf = {}
+        w_q = {}
+        acc2 = {}
+        o_sb = {}
+
+        def stage1(u):
+            r, h = u // 2, u % 2
+            s_codes, s_scales = s_q[r]
+            f_codes, f_scales = u0_q[h]
+            w_bf[u] = wpool.tile([P, 4, P, 4], BF16, name="w_bf", tag="w_bf", align_bytes=64)
+            for g in range(4):
+                bank = ps1.tile([P, 4, P], BANK_DT, name="acc1", tag="acc1")
+                for t in range(4):
+                    nc.tensor.matmul_mx(
+                        out=bank[:, t, :],
+                        lhsT=s_codes[:, P * t : P * (t + 1)].bitcast(FP8X4),
+                        lhsT_scale=s_scales[:, P * t : P * (t + 1)],
+                        rhs=f_codes[:, P * g : P * (g + 1)].bitcast(FP8X4),
+                        rhs_scale=f_scales[:, P * g : P * (g + 1)],
+                        start=True,
+                        stop=True,
+                    )
+                engine = "v" if (u == 0 and g % 2 == 1) else "s"
+                copy_on(engine, w_bf[u][:, g, :, :], bank[:].rearrange("p t n -> p n t"))
+
+        def quantize_w(u):
+            codes = wpool.tile([P, 512], U32, name="w_codes", tag="w_codes", align_bytes=64)
+            scales = wpool.tile([P, 512], U8, name="w_scales", tag="w_scales", align_bytes=64)
+            nc.vector.quantize_mx(
+                out=codes[:].bitcast(FP8X4),
+                scales=scales[:],
+                in_=w_bf[u][:].rearrange("p g n t -> p (g n t)"),
+            )
+            w_q[u] = (codes, scales)
+
+        def stage2(u):
+            codes, scales = w_q[u]
+            u1_codes, u1_scales = u1_q[0]
+            o_sb[u] = opool.tile([P, 4, 512], F32, name="o_sb", tag="o_sb")
+            for g in range(4):
+                bank = ps2.tile([P, 512], F32, name="acc2", tag="acc2")
+                nc.tensor.matmul_mx(
+                    out=bank[:],
+                    lhsT=codes[:, P * g : P * (g + 1)].bitcast(FP8X4),
+                    lhsT_scale=scales[:, P * g : P * (g + 1)],
+                    rhs=u1_codes[:].bitcast(FP8X4),
+                    rhs_scale=u1_scales[:],
+                    start=True,
+                    stop=True,
+                )
+                acc2[(u, g)] = bank
+
+        def out_view(u):
+            r, h = u // 2, u % 2
+            return out[r].rearrange("(n a) i -> n a i", a=N_A)[:, 4 * h : 4 * h + 4, :]
+
+        def drain2(u, g):
+            if u >= N_UNITS - 2:
+                engine = "s" if g % 2 == 1 else "v"
+            else:
+                engine = "s" if (g == 3 and u % 4 != 3) else "v"
+            copy_on(engine, o_sb[u][:, g, :], acc2[(u, g)][:])
+            if u == N_UNITS - 1 and g >= 2:
+                nc.sync.dma_start(out=out_view(u)[:, g : g + 1, :], in_=o_sb[u][:, g : g + 1, :])
+            elif g % 2 == 1:
+                nc.sync.dma_start(out=out_view(u)[:, g - 1 : g + 1, :], in_=o_sb[u][:, g - 1 : g + 1, :])
+
+        u1_q = []
+        quantize_s(0)
+        stage1(0)
+        u1_q.append(prepare_factor(u1_raw, "u1"))
+        stage1(1)
+        quantize_s(1)
+        for u in range(N_UNITS):
+            quantize_w(u)
+            if u % 2 == 1 and (u + 3) // 2 < N_R:
+                quantize_s((u + 3) // 2)
+            if u > 0:
+                drain2(u - 1, 3)
+            stage2(u)
+            if u + 2 < N_UNITS:
+                stage1(u + 2)
+            for g in range(3):
+                drain2(u, g)
+        drain2(N_UNITS - 1, 3)

@@ -18,6 +18,7 @@ N_UNITS = 16
 FLOPS = 2 * 512 * 4096 * 1024 + 2 * 512 * 8192 * 512
 
 S_CHUNK_M = (32, 32, 32, 16, 16)
+WARM_PASSES = (0, 0, 2, 3, 0)
 
 
 def tile_mtl_net_tf_pa_kernel(tc, S, U0, U1, out):
@@ -26,8 +27,8 @@ def tile_mtl_net_tf_pa_kernel(tc, S, U0, U1, out):
         keep = ctx.enter_context(tc.tile_pool(name="keep", bufs=1))
         wpool = ctx.enter_context(tc.tile_pool(name="wpool", bufs=3))
         opool = ctx.enter_context(tc.tile_pool(name="opool", bufs=4))
-        ps1 = ctx.enter_context(tc.psum_pool(name="ps1", bufs=4))
-        ps2 = ctx.enter_context(tc.psum_pool(name="ps2", bufs=4))
+        ps1 = ctx.enter_context(tc.psum_pool(name="ps1", bufs=5))
+        ps2 = ctx.enter_context(tc.psum_pool(name="ps2", bufs=3))
 
         def copy_on(engine, dst, src):
             if engine == "v":
@@ -86,6 +87,15 @@ def tile_mtl_net_tf_pa_kernel(tc, S, U0, U1, out):
         s_grp = [keep.tile([P, 4, 4, P, 4], BF16, name="s_grp%d" % rh, align_bytes=64) for rh in range(2)]
         m0 = 0
         for k, mc in enumerate(S_CHUNK_M):
+            for rep in range(WARM_PASSES[k]):
+                warm_bank = ps2.tile([P, 512], F32, name="warm_bank", tag="acc2")
+                nc.tensor.matmul(
+                    out=warm_bank[:],
+                    lhsT=u0_raw[0][:, 0, 0:P],
+                    rhs=s_raw[k][:, 0, 0:512],
+                    start=True,
+                    stop=True,
+                )
             src5 = s_raw[k][:].rearrange("p j (m t r) -> p j m t r", t=4, r=N_R)
             for rh in range(2):
                 for t in range(4):

from contextlib import ExitStack

import concourse.masks as masks
import concourse.mybir as mybir

F32 = mybir.dt.float32
BF16 = mybir.dt.bfloat16
U32 = mybir.dt.uint32
U8 = mybir.dt.uint8
FP8X4 = mybir.dt.float8_e4m3fn_x4

BANK_DT = F32

P = 128
N_R = 8
N_A = 8
N_UNITS = 16
FLOPS = 2 * 512 * 4096 * 1024 + 2 * 512 * 8192 * 512

S_CHUNK_M = (32, 32, 32, 16, 16)
WARM_PASSES = (0, 0, 2, 3, 0)


def tile_mtl_net_tf_pa_kernel(tc, S, U0, U1, out):
    nc = tc.nc
    with ExitStack() as ctx:
        keep = ctx.enter_context(tc.tile_pool(name="keep", bufs=1))
        wpool = ctx.enter_context(tc.tile_pool(name="wpool", bufs=3))
        opool = ctx.enter_context(tc.tile_pool(name="opool", bufs=4))
        ps1 = ctx.enter_context(tc.psum_pool(name="ps1", bufs=5))
        ps2 = ctx.enter_context(tc.psum_pool(name="ps2", bufs=3))

        def copy_on(engine, dst, src):
            if engine == "v":
                nc.vector.tensor_copy(out=dst, in_=src)
            else:
                nc.scalar.copy(out=dst, in_=src)

        u0_view = U0.rearrange("(m a) q -> m a q", a=N_A)
        u0_raw = []
        for h in range(2):
            t_raw = keep.tile([P, 4, 512], BF16, name="u0_raw%d" % h)
            nc.sync.dma_start(out=t_raw[:], in_=u0_view[:, 4 * h : 4 * h + 4, :])
            u0_raw.append(t_raw)
        s_view = S.rearrange("(k j) p r -> k j (p r)", j=4)
        s_raw = []
        u1_raw = keep.tile([P, 4, 512], BF16, name="u1_raw")
        m0 = 0
        for k, mc in enumerate(S_CHUNK_M):
            t_raw = keep.tile([P, 4, 32 * mc], BF16, name="s_raw%d" % k)
            nc.sync.dma_start(out=t_raw[:], in_=s_view[:, :, 32 * m0 : 32 * (m0 + mc)])
            s_raw.append(t_raw)
            m0 += mc
        nc.sync.dma_start(out=u1_raw[:], in_=U1.rearrange("(b m) k -> m b k", b=4))

        ident = keep.tile([P, P], F32, name="ident")
        masks.make_identity(nc, ident[:])
        warm_in = keep.tile([P, 8], F32, name="warm_in")
        warm_out = keep.tile([P, 8], F32, name="warm_out")
        nc.vector.memset(warm_in[:], 0.0)
        nc.scalar.copy(out=warm_out[:], in_=warm_in[:])

        def prepare_factor(raw, label):
            words = raw[:].bitcast(F32)
            grouped = keep.tile([P, 4, P, 4], BF16, name="grp_" + label, align_bytes=64)
            grouped_words = grouped[:].bitcast(F32)
            for pair in range(2):
                xt = ps2.tile([P, 2, 2, P], F32, name="xt", tag="acc2")
                for s in range(2):
                    for u in range(2):
                        nc.tensor.transpose(xt[:, s, u, :], words[:, 2 * pair + s, u:256:2], ident[:])
                nc.scalar.copy(
                    out=grouped_words[:, 2 * pair : 2 * pair + 2, :, :],
                    in_=xt[:].rearrange("p s u m -> p s m u"),
                )
            codes = keep.tile([P, 512], U32, name="codes_" + label, align_bytes=64)
            scales = keep.tile([P, 512], U8, name="scales_" + label, align_bytes=64)
            nc.vector.quantize_mx(
                out=codes[:].bitcast(FP8X4),
                scales=scales[:],
                in_=grouped[:].rearrange("p s m t -> p (s m t)"),
            )
            return codes, scales

        u0_q = [prepare_factor(u0_raw[0], "u0a"), prepare_factor(u0_raw[1], "u0b")]

        s_grp = [keep.tile([P, 4, 4, P, 4], BF16, name="s_grp%d" % rh, align_bytes=64) for rh in range(2)]
        m0 = 0
        for k, mc in enumerate(S_CHUNK_M):
            for rep in range(WARM_PASSES[k]):
                warm_bank = ps2.tile([P, 512], F32, name="warm_bank", tag="acc2")
                nc.tensor.matmul(
                    out=warm_bank[:],
                    lhsT=u0_raw[0][:, 0, 0:P],
                    rhs=s_raw[k][:, 0, 0:512],
                    start=True,
                    stop=True,
                )
            src5 = s_raw[k][:].rearrange("p j (m t r) -> p j m t r", t=4, r=N_R)
            for rh in range(2):
                for t in range(4):
                    engine = "s" if (t == 3 or (t == 2 and rh == 1 and k % 2 == 0)) else "v"
                    copy_on(
                        engine,
                        s_grp[rh][:, :, t, m0 : m0 + mc, :].rearrange("p r m j -> p m r j"),
                        src5[:, :, :, t, 4 * rh : 4 * rh + 4].rearrange("p j m r -> p m r j"),
                    )
            m0 += mc

        s_q = {}

        def quantize_s(r):
            codes = keep.tile([P, 512], U32, name="s_codes%d" % r, align_bytes=64)
            scales = keep.tile([P, 512], U8, name="s_scales%d" % r, align_bytes=64)
            nc.vector.quantize_mx(
                out=codes[:].bitcast(FP8X4),
                scales=scales[:],
                in_=s_grp[r // 4][:, r % 4, :, :, :].rearrange("p t m j -> p (t m j)"),
            )
            s_q[r] = (codes, scales)

        w_bf = {}
        w_q = {}
        acc2 = {}
        o_sb = {}

        def stage1(u):
            r, h = u // 2, u % 2
            s_codes, s_scales = s_q[r]
            f_codes, f_scales = u0_q[h]
            w_bf[u] = wpool.tile([P, 4, P, 4], BF16, name="w_bf", tag="w_bf", align_bytes=64)
            for g in range(4):
                bank = ps1.tile([P, 4, P], BANK_DT, name="acc1", tag="acc1")
                for t in range(4):
                    nc.tensor.matmul_mx(
                        out=bank[:, t, :],
                        lhsT=s_codes[:, P * t : P * (t + 1)].bitcast(FP8X4),
                        lhsT_scale=s_scales[:, P * t : P * (t + 1)],
                        rhs=f_codes[:, P * g : P * (g + 1)].bitcast(FP8X4),
                        rhs_scale=f_scales[:, P * g : P * (g + 1)],
                        start=True,
                        stop=True,
                    )
                engine = "v" if (u == 0 and g % 2 == 1) else "s"
                copy_on(engine, w_bf[u][:, g, :, :], bank[:].rearrange("p t n -> p n t"))

        def quantize_w(u):
            codes = wpool.tile([P, 512], U32, name="w_codes", tag="w_codes", align_bytes=64)
            scales = wpool.tile([P, 512], U8, name="w_scales", tag="w_scales", align_bytes=64)
            nc.vector.quantize_mx(
                out=codes[:].bitcast(FP8X4),
                scales=scales[:],
                in_=w_bf[u][:].rearrange("p g n t -> p (g n t)"),
            )
            w_q[u] = (codes, scales)

        def stage2(u):
            codes, scales = w_q[u]
            u1_codes, u1_scales = u1_q[0]
            o_sb[u] = opool.tile([P, 4, 512], F32, name="o_sb", tag="o_sb")
            for g in range(4):
                bank = ps2.tile([P, 512], F32, name="acc2", tag="acc2")
                nc.tensor.matmul_mx(
                    out=bank[:],
                    lhsT=codes[:, P * g : P * (g + 1)].bitcast(FP8X4),
                    lhsT_scale=scales[:, P * g : P * (g + 1)],
                    rhs=u1_codes[:].bitcast(FP8X4),
                    rhs_scale=u1_scales[:],
                    start=True,
                    stop=True,
                )
                acc2[(u, g)] = bank

        def out_view(u):
            r, h = u // 2, u % 2
            return out[r].rearrange("(n a) i -> n a i", a=N_A)[:, 4 * h : 4 * h + 4, :]

        def drain2(u, g):
            if u >= N_UNITS - 2:
                engine = "s" if g % 2 == 1 else "v"
            else:
                engine = "s" if (g == 3 and u % 4 != 3) else "v"
            copy_on(engine, o_sb[u][:, g, :], acc2[(u, g)][:])
            if u == N_UNITS - 1 and g >= 2:
                nc.sync.dma_start(out=out_view(u)[:, g : g + 1, :], in_=o_sb[u][:, g : g + 1, :])
            elif g % 2 == 1:
                nc.sync.dma_start(out=out_view(u)[:, g - 1 : g + 1, :], in_=o_sb[u][:, g - 1 : g + 1, :])

        u1_q = []
        quantize_s(0)
        stage1(0)
        u1_q.append(prepare_factor(u1_raw, "u1"))
        stage1(1)
        quantize_s(1)
        for u in range(N_UNITS):
            quantize_w(u)
            if u % 2 == 1 and (u + 3) // 2 < N_R:
                quantize_s((u + 3) // 2)
            if u > 0:
                drain2(u - 1, 3)
            stage2(u)
            if u + 2 < N_UNITS:
                stage1(u + 2)
            for g in range(3):
                drain2(u, g)
        drain2(N_UNITS - 1, 3)
